import numpy as np
import ml_dtypes


def mxq(x, axis, fmt="e4m3"):
    dtype, down = {"e4m3": (ml_dtypes.float8_e4m3fn, 7), "e5m2": (ml_dtypes.float8_e5m2, 14)}[fmt]
    v = np.moveaxis(np.asarray(x, np.float32).astype(ml_dtypes.bfloat16).astype(np.float64), axis, -1)
    blocks = v.reshape(v.shape[:-1] + (-1, 32))
    amax = np.abs(blocks).max(-1, keepdims=True)
    byte = np.maximum(np.where(amax > 0, np.frexp(amax)[1] - 1 + 127, 0) - down, 1)
    scale = np.exp2(byte - 127.0)
    codes = (blocks / scale).astype(np.float32).astype(dtype).astype(np.float64)
    return np.moveaxis((codes * scale).reshape(v.shape), -1, axis)


WIDE = False


def mx_kscale(k):
    if not WIDE:
        return np.ones(k)
    levels = np.array([10, -10, 5, -5, 0])
    if k % 512:
        return np.exp2(np.random.permutation(np.resize(levels, k // 32))).repeat(32)
    a = np.empty((k // 512, 16))
    for p in range(k // 512):
        a[p, :8] = np.random.permutation(np.resize(levels, 8))
        for g in range(8):
            far = levels[np.abs(levels - a[p, g]) >= 10]
            a[p, g + 8] = far[np.random.randint(len(far))]
    return np.exp2(a.ravel()).repeat(32)


BF16 = ml_dtypes.bfloat16


def bf(x):
    return np.asarray(x, np.float32).astype(BF16)


def f64(x):
    return np.asarray(x).astype(np.float64)


B, N, K, H, C_E, M = 2, 64, 16, 1024, 1024, 1024
SCALE = 30.0


def setup_inputs():
    s = mx_kscale(M)
    return {"h2": bf(np.random.standard_normal((B, N, K, M)) * 0.65 * s),
            "h_V": bf(np.random.standard_normal((B, N, H))),
            "mask_attend": bf(np.random.uniform(size=(B, N, K)) < 0.9),
            "W3_w": bf(np.random.standard_normal((M, H)) * 4.0 / np.sqrt(M) / s[:, None]),
            "W3_b": bf(np.random.standard_normal(H) * 0.1)}


def reference(h2, h_V, mask_attend, W3_w, W3_b):
    h_message = (mxq(f64(h2), 3, "e4m3") @ mxq(f64(W3_w), 0, "e4m3")) + f64(W3_b)
    h_message = f64(mask_attend)[..., None] * h_message
    dh = np.sum(h_message, axis=-2) / SCALE
    return f64(h_V) + dh

@@ -1,0 +1,204 @@
+from contextlib import ExitStack
+
+import concourse.mybir as mybir
+from concourse.masks import make_identity
+
+F32 = mybir.dt.float32
+BF16 = mybir.dt.bfloat16
+U32 = mybir.dt.uint32
+U8 = mybir.dt.uint8
+FP8X4 = mybir.dt.float8_e4m3fn_x4
+ALU = mybir.AluOpType
+
+P = 128
+EDGES = 16
+K = 1024
+H = 1024
+PACK = 4
+K_PASS = P * PACK
+PASSES = K // K_PASS
+PLANES = K // (2 * P)
+N_TILE = 512
+HALVES = H // N_TILE
+GROUPS = ((0, 512), (512, 256), (768, 256))
+CHUNK = 4
+CHUNKS = EDGES // CHUNK
+LOAD = 2
+LAG = 2
+SCALE = 30.0
+
+FLOPS = 2 * P * EDGES * K * H
+
+
+def tile_declayerj_pb_kernel(tc, h2, h_V, mask_attend, W3_w, W3_b, out):
+    nc = tc.nc
+    h2_rows = h2.rearrange("b n e k -> (b n) (e k)")
+    mask_rows = mask_attend.rearrange("b n e -> (b n) e")
+    hv_rows = h_V.rearrange("b n h -> (b n) h")
+    out_rows = out.rearrange("b n h -> (b n) h")
+
+    with ExitStack() as ctx:
+        keep = ctx.enter_context(tc.tile_pool(name="keep", bufs=1))
+        acc_pool = ctx.enter_context(tc.psum_pool(name="acc", bufs=1))
+        turn_pool = ctx.enter_context(tc.psum_pool(name="turn", bufs=CHUNK))
+        ctx.enter_context(tc.manual_schedule())
+
+        mask_bf = keep.tile([P, EDGES], BF16)
+        nc.sync.dma_start(out=mask_bf[:], in_=mask_rows)
+
+        bias_rows = keep.tile([P, H], BF16)
+        nc.vector.memset(bias_rows[:], 0.0)
+        nc.scalar.dma_start(out=bias_rows[0:1, :], in_=W3_b.unsqueeze(0))
+        ones = keep.tile([P, P], BF16)
+        nc.vector.memset(ones[:], 1.0)
+
+        w_raw = [keep.tile([P, PASSES, PACK, N_TILE], BF16, name="w_raw%d" % half) for half in range(HALVES)]
+        h2_in = [keep.tile([P, CHUNK * K], BF16, name="h2_in%d" % c) for c in range(CHUNKS)]
+
+        def load_w(half, g):
+            nc.sync.dma_start(
+                out=w_raw[half][:, g],
+                in_=W3_w[K_PASS * g : K_PASS * (g + 1), N_TILE * half : N_TILE * (half + 1)].rearrange(
+                    "(p t) c -> p t c", t=PACK
+                ),
+            )
+
+        def load_h2(c):
+            for first in range(0, CHUNK * K, LOAD * K):
+                nc.sync.dma_start(
+                    out=h2_in[c][:, first : first + LOAD * K],
+                    in_=h2_rows[:, CHUNK * K * c + first : CHUNK * K * c + first + LOAD * K],
+                )
+
+        for g in range(PASSES):
+            load_w(0, g)
+        for c in range(CHUNKS):
+            load_h2(c)
+            if 0 <= c - 1 < PASSES:
+                load_w(1, c - 1)
+        hv = keep.tile([P, H], BF16)
+        nc.sync.dma_start(out=hv[:], in_=hv_rows)
+
+        ident = keep.tile([P, P], F32)
+        make_identity(nc, ident[:])
+        mask_f32 = keep.tile([P, EDGES], F32)
+        nc.vector.tensor_copy(out=mask_f32[:], in_=mask_bf[:])
+        gates = keep.tile([P, EDGES, P], F32)
+
+        def make_gates(c):
+            for e in range(CHUNK * c, CHUNK * (c + 1)):
+                nc.vector.tensor_scalar(
+                    out=gates[:, e, :], in0=ident[:], scalar1=mask_f32[:, e : e + 1], scalar2=None, op0=ALU.mult
+                )
+
+        make_gates(0)
+
+        count = keep.tile([P, 1], F32)
+        nc.vector.reduce_sum(out=count[:], in_=mask_f32[:], axis=mybir.AxisListType.X)
+        count30 = keep.tile([P, 1], F32)
+        nc.vector.tensor_scalar(out=count30[:], in0=count[:], scalar1=1.0 / SCALE, scalar2=None, op0=ALU.mult)
+
+        bias_all = [acc_pool.tile([P, N_TILE], F32, name="bias_all%d" % half, tag="late%d" % half) for half in range(HALVES)]
+        for half in range(HALVES):
+            nc.tensor.matmul(
+                out=bias_all[half][:],
+                lhsT=ones[:],
+                rhs=bias_rows[:, N_TILE * half : N_TILE * (half + 1)],
+                start=True,
+                stop=True,
+            )
+
+        w_grouped = [
+            keep.tile([P, PASSES, N_TILE, PACK], BF16, name="w_grouped%d" % half, align_bytes=64)
+            for half in range(HALVES)
+        ]
+        w_codes = keep.tile([P, PASSES, H], U32, align_bytes=64)
+        w_scales = keep.tile([P, PASSES, H], U8, align_bytes=64)
+
+        def regroup_w(half, g):
+            nc.vector.tensor_copy(
+                out=w_grouped[half][:, g].rearrange("p (c i) t -> p c t i", i=4),
+                in_=w_raw[half][:, g].rearrange("p t (c i) -> p c t i", i=4),
+            )
+
+        def quantise_w(half, g):
+            cols = slice(N_TILE * half, N_TILE * (half + 1))
+            nc.vector.quantize_mx(
+                out=w_codes[:, g, cols].bitcast(FP8X4),
+                scales=w_scales[:, g, cols],
+                in_=w_grouped[half][:, g].rearrange("p c t -> p (c t)"),
+            )
+
+        h2_grouped = [keep.tile([P, CHUNK * K], BF16, name="h2_grouped%d" % c, align_bytes=64) for c in range(CHUNKS)]
+        h2_codes = keep.tile([P, EDGES, PASSES * P], U32, align_bytes=64)
+        h2_scales = keep.tile([P, EDGES, PASSES * P], U8, align_bytes=64)
+
+        def quantise_h2(c):
+            words_in = h2_in[c][:].bitcast(F32)
+            words_out = h2_grouped[c][:].bitcast(F32).rearrange(
+                "p (e g n u) -> p e g n u", e=CHUNK, g=PASSES, u=2
+            )
+            for i in range(CHUNK):
+                e = CHUNK * c + i
+                turned = turn_pool.tile([P, PLANES, P], F32)
+                for j in range(PLANES):
+                    first = PLANES * P * i + 2 * P * (j // 2) + j % 2
+                    nc.tensor.transpose(turned[:, j, :], words_in[:, first : first + 2 * P - 1 : 2], gates[:, e, :])
+                nc.scalar.copy(out=words_out[:, i], in_=turned[:].rearrange("p (g u) n -> p g n u", u=2))
+                nc.vector.quantize_mx(
+                    out=h2_codes[:, e, :].bitcast(FP8X4),
+                    scales=h2_scales[:, e, :],
+                    in_=h2_grouped[c][:, K * i : K * (i + 1)],
+                )
+
+        def multiply(acc, group, edges):
+            first, width = group
+            for e in edges:
+                for g in range(PASSES):
+                    nc.tensor.matmul_mx(
+                        out=acc[:],
+                        lhsT=h2_codes[:, e, P * g : P * (g + 1)].bitcast(FP8X4),
+                        lhsT_scale=h2_scales[:, e, P * g : P * (g + 1)],
+                        rhs=w_codes[:, g, first : first + width].bitcast(FP8X4),
+                        rhs_scale=w_scales[:, g, first : first + width],
+                        start=(e == 0 and g == 0),
+                        stop=(e == EDGES - 1 and g == PASSES - 1),
+                    )
+
+        base = keep.tile([P, H], F32)
+        result = keep.tile([P, H], F32)
+
+        def finish(acc, group):
+            first, width = group
+            cols = slice(first, first + width)
+            nc.vector.scalar_tensor_tensor(
+                out=result[:, cols], in0=acc[:], scalar=1.0 / SCALE, in1=base[:, cols], op0=ALU.mult, op1=ALU.add
+            )
+            nc.sync.dma_start(out=out_rows[:, cols], in_=result[:, cols])
+
+        for g in range(PASSES):
+            regroup_w(0, g)
+        for g in range(PASSES):
+            quantise_w(0, g)
+        acc_first = acc_pool.tile([P, GROUPS[0][1]], F32)
+        for c in range(CHUNKS):
+            if c + 1 < CHUNKS:
+                make_gates(c + 1)
+            quantise_h2(c)
+            if 0 <= c - 1 < PASSES:
+                regroup_w(1, c - 1)
+                quantise_w(1, c - 1)
+            multiply(acc_first, GROUPS[0], range(max(0, CHUNK * c - LAG), CHUNK * (c + 1) - LAG))
+        multiply(acc_first, GROUPS[0], range(EDGES - LAG, EDGES))
+
+        for half in range(HALVES):
+            cols = slice(N_TILE * half, N_TILE * (half + 1))
+            nc.vector.scalar_tensor_tensor(
+                out=base[:, cols], in0=bias_all[half][:], scalar=count30[:, 0:1], in1=hv[:, cols], op0=ALU.mult, op1=ALU.add
+            )
+        finish(acc_first, GROUPS[0])
+
+        for late, group in enumerate(GROUPS[1:]):
+            acc_late = acc_pool.tile([P, group[1]], F32, tag="late%d" % late)
+            multiply(acc_late, group, range(EDGES))
+            finish(acc_late, group)

@@ -9,22 +9,20 @@ U32 = mybir.dt.uint32
 U8 = mybir.dt.uint8
 FP8X4 = mybir.dt.float8_e4m3fn_x4
 ALU = mybir.AluOpType
+ACT = mybir.ActivationFunctionType
 
 P = 128
 EDGES = 16
 K = 1024
 H = 1024
 PACK = 4
-K_PASS = P * PACK
-PASSES = K // K_PASS
-PLANES = K // (2 * P)
-N_TILE = 512
-HALVES = H // N_TILE
-GROUPS = ((0, 512), (512, 256), (768, 256))
-CHUNK = 4
-CHUNKS = EDGES // CHUNK
-LOAD = 2
-LAG = 2
+K_HALF = P * PACK
+HALVES = 2
+N_HALF = H // HALVES
+GROUPS = ((0, 256), (256, 256), (512, 256), (768, 256))
+LATE = 2
+PAIR = 2
+RUN = 4
 SCALE = 30.0
 
 FLOPS = 2 * P * EDGES * K * H
@@ -32,7 +30,7 @@ FLOPS = 2 * P * EDGES * K * H
 
 def tile_declayerj_pb_kernel(tc, h2, h_V, mask_attend, W3_w, W3_b, out):
     nc = tc.nc
-    h2_rows = h2.rearrange("b n e k -> (b n) (e k)")
+    h2_rows = h2.rearrange("b n e k -> (b n) e k")
     mask_rows = mask_attend.rearrange("b n e -> (b n) e")
     hv_rows = h_V.rearrange("b n h -> (b n) h")
     out_rows = out.rearrange("b n h -> (b n) h")
@@ -40,42 +38,52 @@ def tile_declayerj_pb_kernel(tc, h2, h_V, mask_attend, W3_w, W3_b, out):
     with ExitStack() as ctx:
         keep = ctx.enter_context(tc.tile_pool(name="keep", bufs=1))
         acc_pool = ctx.enter_context(tc.psum_pool(name="acc", bufs=1))
-        turn_pool = ctx.enter_context(tc.psum_pool(name="turn", bufs=CHUNK))
+        turn_pool = ctx.enter_context(tc.psum_pool(name="turn", bufs=4))
         ctx.enter_context(tc.manual_schedule())
 
-        mask_bf = keep.tile([P, EDGES], BF16)
-        nc.sync.dma_start(out=mask_bf[:], in_=mask_rows)
-
         bias_rows = keep.tile([P, H], BF16)
-        nc.vector.memset(bias_rows[:], 0.0)
-        nc.scalar.dma_start(out=bias_rows[0:1, :], in_=W3_b.unsqueeze(0))
+        nc.gpsimd.memset(bias_rows[:].bitcast(F32), 0.0)
         ones = keep.tile([P, P], BF16)
         nc.vector.memset(ones[:], 1.0)
+        mask_bf = keep.tile([P, EDGES], BF16)
+        nc.scalar.dma_start(out=mask_bf[:], in_=mask_rows)
+        nc.scalar.dma_start(out=bias_rows[0:1, :], in_=W3_b.unsqueeze(0))
+        warm = keep.tile([P, 1], F32)
+        nc.scalar.copy(out=warm[:], in_=ones[:, 0:1])
 
-        w_raw = [keep.tile([P, PASSES, PACK, N_TILE], BF16, name="w_raw%d" % half) for half in range(HALVES)]
-        h2_in = [keep.tile([P, CHUNK * K], BF16, name="h2_in%d" % c) for c in range(CHUNKS)]
+        w_raw = {}
+        h2_in = {}
 
-        def load_w(half, g):
+        def load_w(g, first, width):
+            w_raw[g, first] = keep.tile([P, PACK, width], BF16, name="w_raw%d_%d" % (g, first))
             nc.sync.dma_start(
-                out=w_raw[half][:, g],
-                in_=W3_w[K_PASS * g : K_PASS * (g + 1), N_TILE * half : N_TILE * (half + 1)].rearrange(
-                    "(p t) c -> p t c", t=PACK
-                ),
+                out=w_raw[g, first][:],
+                in_=W3_w[K_HALF * g : K_HALF * (g + 1), first : first + width].rearrange("(p t) c -> p t c", t=PACK),
             )
 
-        def load_h2(c):
-            for first in range(0, CHUNK * K, LOAD * K):
-                nc.sync.dma_start(
-                    out=h2_in[c][:, first : first + LOAD * K],
-                    in_=h2_rows[:, CHUNK * K * c + first : CHUNK * K * c + first + LOAD * K],
-                )
+        def load_h2(g, first, edges):
+            piece = keep.tile([P, edges, K_HALF], BF16, name="h2_in%d_%d" % (g, first))
+            for i in range(edges):
+                h2_in[g, first + i] = piece[:, i, :]
+            nc.sync.dma_start(
+                out=piece[:],
+                in_=h2_rows[:, first : first + edges, K_HALF * g : K_HALF * (g + 1)],
+            )
 
-        for g in range(PASSES):
-            load_w(0, g)
-        for c in range(CHUNKS):
-            load_h2(c)
-            if 0 <= c - 1 < PASSES:
-                load_w(1, c - 1)
+        load_h2(0, 0, 2)
+        load_w(0, 0, 256)
+        load_w(0, 256, 256)
+        load_h2(0, 2, 2)
+        load_w(0, 512, 512)
+        load_h2(0, 4, 4)
+        load_h2(0, 8, 4)
+        load_w(1, 0, 512)
+        load_h2(0, 12, 4)
+        load_h2(1, 0, 4)
+        load_w(1, 512, 512)
+        load_h2(1, 4, 4)
+        load_h2(1, 8, 4)
+        load_h2(1, 12, 4)
         hv = keep.tile([P, H], BF16)
         nc.sync.dma_start(out=hv[:], in_=hv_rows)
 
@@ -85,120 +93,151 @@ def tile_declayerj_pb_kernel(tc, h2, h_V, mask_attend, W3_w, W3_b, out):
         nc.vector.tensor_copy(out=mask_f32[:], in_=mask_bf[:])
         gates = keep.tile([P, EDGES, P], F32)
 
-        def make_gates(c):
-            for e in range(CHUNK * c, CHUNK * (c + 1)):
-                nc.vector.tensor_scalar(
-                    out=gates[:, e, :], in0=ident[:], scalar1=mask_f32[:, e : e + 1], scalar2=None, op0=ALU.mult
-                )
+        for e in range(EDGES // 2):
+            nc.vector.tensor_scalar(
+                out=gates[:, e, :], in0=ident[:], scalar1=mask_f32[:, e : e + 1], scalar2=None, op0=ALU.mult
+            )
 
-        make_gates(0)
+        def make_late_gates():
+            for e in range(EDGES // 2, EDGES):
+                nc.scalar.activation(out=gates[:, e, :], in_=ident[:], func=ACT.Copy, scale=mask_f32[:, e : e + 1])
 
         count = keep.tile([P, 1], F32)
         nc.vector.reduce_sum(out=count[:], in_=mask_f32[:], axis=mybir.AxisListType.X)
         count30 = keep.tile([P, 1], F32)
         nc.vector.tensor_scalar(out=count30[:], in0=count[:], scalar1=1.0 / SCALE, scalar2=None, op0=ALU.mult)
 
-        bias_all = [acc_pool.tile([P, N_TILE], F32, name="bias_all%d" % half, tag="late%d" % half) for half in range(HALVES)]
-        for half in range(HALVES):
-            nc.tensor.matmul(
-                out=bias_all[half][:],
-                lhsT=ones[:],
-                rhs=bias_rows[:, N_TILE * half : N_TILE * (half + 1)],
-                start=True,
-                stop=True,
-            )
+        base = keep.tile([P, H], F32)
 
-        w_grouped = [
-            keep.tile([P, PASSES, N_TILE, PACK], BF16, name="w_grouped%d" % half, align_bytes=64)
-            for half in range(HALVES)
-        ]
-        w_codes = keep.tile([P, PASSES, H], U32, align_bytes=64)
-        w_scales = keep.tile([P, PASSES, H], U8, align_bytes=64)
+        def spread_bias():
+            for half in range(HALVES):
+                cols = slice(N_HALF * half, N_HALF * (half + 1))
+                spread = turn_pool.tile([P, N_HALF], F32, tag="turn")
+                nc.tensor.matmul(out=spread[:], lhsT=ones[:], rhs=bias_rows[:, cols], start=True, stop=True)
+                nc.scalar.activation(out=base[:, cols], in_=spread[:], func=ACT.Copy, scale=count30[:, 0:1])
 
-        def regroup_w(half, g):
+        w_codes = keep.tile([P, HALVES, H], U32, align_bytes=64)
+        w_scales = keep.tile([P, HALVES, H], U8, align_bytes=64)
+        w_grouped = {}
+
+        def regroup_w(g, first):
+            raw = w_raw[g, first]
+            width = raw.shape[2]
+            grouped = keep.tile([P, width, PACK], BF16, name="w_grouped%d_%d" % (g, first), align_bytes=64)
+            w_grouped[g, first] = grouped
             nc.vector.tensor_copy(
-                out=w_grouped[half][:, g].rearrange("p (c i) t -> p c t i", i=4),
-                in_=w_raw[half][:, g].rearrange("p t (c i) -> p c t i", i=4),
+                out=grouped[:].rearrange("p (c i) t -> p c t i", i=4),
+                in_=raw[:].rearrange("p t (c i) -> p c t i", i=4),
             )
 
-        def quantise_w(half, g):
-            cols = slice(N_TILE * half, N_TILE * (half + 1))
+        def quantise_w(g, first):
+            grouped = w_grouped[g, first]
+            cols = slice(first, first + grouped.shape[1])
             nc.vector.quantize_mx(
                 out=w_codes[:, g, cols].bitcast(FP8X4),
                 scales=w_scales[:, g, cols],
-                in_=w_grouped[half][:, g].rearrange("p c t -> p (c t)"),
+                in_=grouped[:].rearrange("p c t -> p (c t)"),
             )
 
-        h2_grouped = [keep.tile([P, CHUNK * K], BF16, name="h2_grouped%d" % c, align_bytes=64) for c in range(CHUNKS)]
-        h2_codes = keep.tile([P, EDGES, PASSES * P], U32, align_bytes=64)
-        h2_scales = keep.tile([P, EDGES, PASSES * P], U8, align_bytes=64)
+        h2_codes = keep.tile([P, HALVES, EDGES * P], U32, align_bytes=64)
+        h2_scales = keep.tile([P, HALVES, EDGES * P], U8, align_bytes=64)
 
-        def quantise_h2(c):
-            words_in = h2_in[c][:].bitcast(F32)
-            words_out = h2_grouped[c][:].bitcast(F32).rearrange(
-                "p (e g n u) -> p e g n u", e=CHUNK, g=PASSES, u=2
-            )
-            for i in range(CHUNK):
-                e = CHUNK * c + i
-                turned = turn_pool.tile([P, PLANES, P], F32)
-                for j in range(PLANES):
-                    first = PLANES * P * i + 2 * P * (j // 2) + j % 2
-                    nc.tensor.transpose(turned[:, j, :], words_in[:, first : first + 2 * P - 1 : 2], gates[:, e, :])
-                nc.scalar.copy(out=words_out[:, i], in_=turned[:].rearrange("p (g u) n -> p g n u", u=2))
+        h2_grouped = {}
+
+        def turn_h2(g, first, edges=RUN):
+            for pair in range(first, first + edges, PAIR):
+                turned = turn_pool.tile([P, PAIR, 2, P], F32, tag="turn")
+                for i in range(PAIR):
+                    e = pair + i
+                    words = h2_in[g, e].bitcast(F32)
+                    for u in range(2):
+                        nc.tensor.transpose(turned[:, i, u, :], words[:, u : u + 2 * P - 1 : 2], gates[:, e, :])
+                grouped = keep.tile([P, PAIR * P * PACK], BF16, name="h2_grouped%d_%d" % (g, pair), align_bytes=64)
+                nc.scalar.copy(
+                    out=grouped[:].bitcast(F32).rearrange("p (e n u) -> p e n u", e=PAIR, u=2),
+                    in_=turned[:].rearrange("p e u n -> p e n u"),
+                )
+                h2_grouped[g, pair] = grouped
+
+        def quantise_h2(g, first, edges=RUN):
+            for pair in range(first, first + edges, PAIR):
                 nc.vector.quantize_mx(
-                    out=h2_codes[:, e, :].bitcast(FP8X4),
-                    scales=h2_scales[:, e, :],
-                    in_=h2_grouped[c][:, K * i : K * (i + 1)],
+                    out=h2_codes[:, g, P * pair : P * (pair + PAIR)].bitcast(FP8X4),
+                    scales=h2_scales[:, g, P * pair : P * (pair + PAIR)],
+                    in_=h2_grouped[g, pair][:],
                 )
 
-        def multiply(acc, group, edges):
-            first, width = group
-            for e in edges:
-                for g in range(PASSES):
-                    nc.tensor.matmul_mx(
-                        out=acc[:],
-                        lhsT=h2_codes[:, e, P * g : P * (g + 1)].bitcast(FP8X4),
-                        lhsT_scale=h2_scales[:, e, P * g : P * (g + 1)],
-                        rhs=w_codes[:, g, first : first + width].bitcast(FP8X4),
-                        rhs_scale=w_scales[:, g, first : first + width],
-                        start=(e == 0 and g == 0),
-                        stop=(e == EDGES - 1 and g == PASSES - 1),
-                    )
+        acc = [acc_pool.tile([P, width], F32, name="acc%d" % i) for i, (first, width) in enumerate(GROUPS)]
 
-        base = keep.tile([P, H], F32)
+        def multiply(g, group, edges):
+            first, width = GROUPS[group]
+            for e in edges:
+                nc.tensor.matmul_mx(
+                    out=acc[group][:],
+                    lhsT=h2_codes[:, g, P * e : P * (e + 1)].bitcast(FP8X4),
+                    lhsT_scale=h2_scales[:, g, P * e : P * (e + 1)],
+                    rhs=w_codes[:, g, first : first + width].bitcast(FP8X4),
+                    rhs_scale=w_scales[:, g, first : first + width],
+                    start=(e == 0 and g == 0),
+                    stop=(e == EDGES - 1 and g == HALVES - 1),
+                )
+
         result = keep.tile([P, H], F32)
 
-        def finish(acc, group):
-            first, width = group
+        def finish(group):
+            first, width = GROUPS[group]
             cols = slice(first, first + width)
             nc.vector.scalar_tensor_tensor(
-                out=result[:, cols], in0=acc[:], scalar=1.0 / SCALE, in1=base[:, cols], op0=ALU.mult, op1=ALU.add
+                out=result[:, cols], in0=acc[group][:], scalar=1.0 / SCALE, in1=base[:, cols], op0=ALU.mult, op1=ALU.add
             )
             nc.sync.dma_start(out=out_rows[:, cols], in_=result[:, cols])
 
-        for g in range(PASSES):
-            regroup_w(0, g)
-        for g in range(PASSES):
-            quantise_w(0, g)
-        acc_first = acc_pool.tile([P, GROUPS[0][1]], F32)
-        for c in range(CHUNKS):
-            if c + 1 < CHUNKS:
-                make_gates(c + 1)
-            quantise_h2(c)
-            if 0 <= c - 1 < PASSES:
-                regroup_w(1, c - 1)
-                quantise_w(1, c - 1)
-            multiply(acc_first, GROUPS[0], range(max(0, CHUNK * c - LAG), CHUNK * (c + 1) - LAG))
-        multiply(acc_first, GROUPS[0], range(EDGES - LAG, EDGES))
+        def edges_of(first):
+            return range(first, first + RUN)
 
+        def multiply_all(g, groups, first):
+            for group in groups:
+                multiply(g, group, edges_of(first))
+
+        every, early, late = range(len(GROUPS)), range(LATE), range(LATE, len(GROUPS))
+        spread_bias()
+        regroup_w(0, 0)
+        quantise_w(0, 0)
+        turn_h2(0, 0)
+        quantise_h2(0, 0, PAIR)
+        regroup_w(0, 256)
+        quantise_w(0, 256)
+        quantise_h2(0, PAIR, PAIR)
+        multiply_all(0, early, 0)
+        regroup_w(0, 512)
+        quantise_w(0, 512)
+        turn_h2(0, 4)
+        quantise_h2(0, 4)
+        make_late_gates()
+        multiply_all(0, late, 0)
+        turn_h2(0, 8)
+        quantise_h2(0, 8)
+        regroup_w(1, 0)
+        multiply_all(0, every, 4)
+        turn_h2(0, 12)
+        quantise_h2(0, 12)
+        quantise_w(1, 0)
+        regroup_w(1, 512)
+        multiply_all(0, every, 8)
+        turn_h2(1, 0)
+        quantise_h2(1, 0)
+        quantise_w(1, 512)
+        multiply_all(0, every, 12)
+        for first in range(RUN, EDGES, RUN):
+            turn_h2(1, first)
+            quantise_h2(1, first)
+            multiply_all(1, early, first - RUN)
+        multiply_all(1, early, EDGES - RUN)
         for half in range(HALVES):
-            cols = slice(N_TILE * half, N_TILE * (half + 1))
-            nc.vector.scalar_tensor_tensor(
-                out=base[:, cols], in0=bias_all[half][:], scalar=count30[:, 0:1], in1=hv[:, cols], op0=ALU.mult, op1=ALU.add
-            )
-        finish(acc_first, GROUPS[0])
-
-        for late, group in enumerate(GROUPS[1:]):
-            acc_late = acc_pool.tile([P, group[1]], F32, tag="late%d" % late)
-            multiply(acc_late, group, range(EDGES))
-            finish(acc_late, group)
+            cols = slice(N_HALF * half, N_HALF * (half + 1))
+            nc.vector.tensor_tensor(out=base[:, cols], in0=base[:, cols], in1=hv[:, cols], op=ALU.add)
+        for group in early:
+            finish(group)
+        for group in late:
+            multiply(1, group, range(EDGES))
+            finish(group)

@@ -19,10 +19,9 @@ PACK = 4
 K_HALF = P * PACK
 HALVES = 2
 N_HALF = H // HALVES
-GROUPS = ((0, 256), (256, 256), (512, 256), (768, 256))
-LATE = 2
+GROUPS = ((0, 512), (512, 256), (768, 256))
+ITEMS = HALVES * EDGES
 PAIR = 2
-RUN = 4
 SCALE = 30.0
 
 FLOPS = 2 * P * EDGES * K * H
@@ -38,13 +37,15 @@ def tile_declayerj_pb_kernel(tc, h2, h_V, mask_attend, W3_w, W3_b, out):
     with ExitStack() as ctx:
         keep = ctx.enter_context(tc.tile_pool(name="keep", bufs=1))
         acc_pool = ctx.enter_context(tc.psum_pool(name="acc", bufs=1))
-        turn_pool = ctx.enter_context(tc.psum_pool(name="turn", bufs=4))
+        turn_pool = ctx.enter_context(tc.psum_pool(name="turn", bufs=5))
         ctx.enter_context(tc.manual_schedule())
 
         bias_rows = keep.tile([P, H], BF16)
         nc.gpsimd.memset(bias_rows[:].bitcast(F32), 0.0)
         ones = keep.tile([P, P], BF16)
         nc.vector.memset(ones[:], 1.0)
+        blank = keep.tile([P, N_HALF], BF16)
+        nc.vector.memset(blank[:].bitcast(F32), 0.0)
         mask_bf = keep.tile([P, EDGES], BF16)
         nc.scalar.dma_start(out=mask_bf[:], in_=mask_rows)
         nc.scalar.dma_start(out=bias_rows[0:1, :], in_=W3_b.unsqueeze(0))
@@ -61,29 +62,27 @@ def tile_declayerj_pb_kernel(tc, h2, h_V, mask_attend, W3_w, W3_b, out):
                 in_=W3_w[K_HALF * g : K_HALF * (g + 1), first : first + width].rearrange("(p t) c -> p t c", t=PACK),
             )
 
-        def load_h2(g, first, edges):
-            piece = keep.tile([P, edges, K_HALF], BF16, name="h2_in%d_%d" % (g, first))
-            for i in range(edges):
-                h2_in[g, first + i] = piece[:, i, :]
+        def load_h2(first, items):
+            piece = keep.tile([P, items, K_HALF], BF16, name="h2_in%d" % first)
+            h2_in[first] = piece
+            g, e = divmod(first, EDGES)
             nc.sync.dma_start(
                 out=piece[:],
-                in_=h2_rows[:, first : first + edges, K_HALF * g : K_HALF * (g + 1)],
+                in_=h2_rows[:, e : e + items, K_HALF * g : K_HALF * (g + 1)],
             )
 
-        load_h2(0, 0, 2)
-        load_w(0, 0, 256)
-        load_w(0, 256, 256)
-        load_h2(0, 2, 2)
+        load_w(0, 0, 512)
+        load_h2(0, 4)
         load_w(0, 512, 512)
-        load_h2(0, 4, 4)
-        load_h2(0, 8, 4)
+        load_h2(4, 4)
+        load_h2(8, 4)
+        load_h2(12, 4)
         load_w(1, 0, 512)
-        load_h2(0, 12, 4)
-        load_h2(1, 0, 4)
+        load_h2(16, 4)
+        load_h2(20, 4)
+        load_h2(24, 4)
         load_w(1, 512, 512)
-        load_h2(1, 4, 4)
-        load_h2(1, 8, 4)
-        load_h2(1, 12, 4)
+        load_h2(28, 4)
         hv = keep.tile([P, H], BF16)
         nc.sync.dma_start(out=hv[:], in_=hv_rows)
 
@@ -93,14 +92,13 @@ def tile_declayerj_pb_kernel(tc, h2, h_V, mask_attend, W3_w, W3_b, out):
         nc.vector.tensor_copy(out=mask_f32[:], in_=mask_bf[:])
         gates = keep.tile([P, EDGES, P], F32)
 
-        for e in range(EDGES // 2):
-            nc.vector.tensor_scalar(
-                out=gates[:, e, :], in0=ident[:], scalar1=mask_f32[:, e : e + 1], scalar2=None, op0=ALU.mult
-            )
+        def make_gates(first, end):
+            for e in range(first, end):
+                nc.vector.tensor_scalar(
+                    out=gates[:, e, :], in0=ident[:], scalar1=mask_f32[:, e : e + 1], scalar2=None, op0=ALU.mult
+                )
 
-        def make_late_gates():
-            for e in range(EDGES // 2, EDGES):
-                nc.scalar.activation(out=gates[:, e, :], in_=ident[:], func=ACT.Copy, scale=mask_f32[:, e : e + 1])
+        make_gates(0, 8)
 
         count = keep.tile([P, 1], F32)
         nc.vector.reduce_sum(out=count[:], in_=mask_f32[:], axis=mybir.AxisListType.X)
@@ -139,48 +137,60 @@ def tile_declayerj_pb_kernel(tc, h2, h_V, mask_attend, W3_w, W3_b, out):
                 in_=grouped[:].rearrange("p c t -> p (c t)"),
             )
 
-        h2_codes = keep.tile([P, HALVES, EDGES * P], U32, align_bytes=64)
-        h2_scales = keep.tile([P, HALVES, EDGES * P], U8, align_bytes=64)
-
+        h2_codes = keep.tile([P, ITEMS, P], U32, align_bytes=64)
+        h2_scales = keep.tile([P, ITEMS, P], U8, align_bytes=64)
         h2_grouped = {}
 
-        def turn_h2(g, first, edges=RUN):
-            for pair in range(first, first + edges, PAIR):
+        planes = {}
+
+        def planes_of(first, order):
+            words = h2_in[first][:].bitcast(F32).rearrange("p i (n u) -> p i u n", u=2)
+            items = words.shape[1]
+            if order:
+                ordered = keep.tile([P, items, 2, P], F32, name="h2_ordered%d" % first)
+                nc.vector.tensor_copy(out=ordered[:], in_=words)
+                words = ordered[:]
+            for i in range(items):
+                planes[first + i] = [words[:, i, u, :] for u in range(2)]
+
+        def turn_h2(first, end):
+            for pair in range(first, end, PAIR):
                 turned = turn_pool.tile([P, PAIR, 2, P], F32, tag="turn")
                 for i in range(PAIR):
-                    e = pair + i
-                    words = h2_in[g, e].bitcast(F32)
+                    gate = gates[:, (pair + i) % EDGES, :]
                     for u in range(2):
-                        nc.tensor.transpose(turned[:, i, u, :], words[:, u : u + 2 * P - 1 : 2], gates[:, e, :])
-                grouped = keep.tile([P, PAIR * P * PACK], BF16, name="h2_grouped%d_%d" % (g, pair), align_bytes=64)
+                        nc.tensor.transpose(turned[:, i, u, :], planes[pair + i][u], gate)
+                grouped = keep.tile([P, PAIR * P * PACK], BF16, name="h2_grouped%d" % pair, align_bytes=64)
                 nc.scalar.copy(
-                    out=grouped[:].bitcast(F32).rearrange("p (e n u) -> p e n u", e=PAIR, u=2),
-                    in_=turned[:].rearrange("p e u n -> p e n u"),
+                    out=grouped[:].bitcast(F32).rearrange("p (i n u) -> p i n u", i=PAIR, u=2),
+                    in_=turned[:].rearrange("p i u n -> p i n u"),
                 )
-                h2_grouped[g, pair] = grouped
+                h2_grouped[pair] = grouped
 
-        def quantise_h2(g, first, edges=RUN):
-            for pair in range(first, first + edges, PAIR):
+        def quantise_h2(first, end):
+            for pair in range(first, end, PAIR):
                 nc.vector.quantize_mx(
-                    out=h2_codes[:, g, P * pair : P * (pair + PAIR)].bitcast(FP8X4),
-                    scales=h2_scales[:, g, P * pair : P * (pair + PAIR)],
-                    in_=h2_grouped[g, pair][:],
+                    out=h2_codes[:, pair : pair + PAIR, :].rearrange("p i n -> p (i n)").bitcast(FP8X4),
+                    scales=h2_scales[:, pair : pair + PAIR, :].rearrange("p i n -> p (i n)"),
+                    in_=h2_grouped[pair][:],
                 )
 
         acc = [acc_pool.tile([P, width], F32, name="acc%d" % i) for i, (first, width) in enumerate(GROUPS)]
 
-        def multiply(g, group, edges):
-            first, width = GROUPS[group]
-            for e in edges:
-                nc.tensor.matmul_mx(
-                    out=acc[group][:],
-                    lhsT=h2_codes[:, g, P * e : P * (e + 1)].bitcast(FP8X4),
-                    lhsT_scale=h2_scales[:, g, P * e : P * (e + 1)],
-                    rhs=w_codes[:, g, first : first + width].bitcast(FP8X4),
-                    rhs_scale=w_scales[:, g, first : first + width],
-                    start=(e == 0 and g == 0),
-                    stop=(e == EDGES - 1 and g == HALVES - 1),
-                )
+        def multiply(groups, items_first, items_end):
+            for group in groups:
+                first, width = GROUPS[group]
+                for n in range(items_first, items_end):
+                    g = n // EDGES
+                    nc.tensor.matmul_mx(
+                        out=acc[group][:],
+                        lhsT=h2_codes[:, n, :].bitcast(FP8X4),
+                        lhsT_scale=h2_scales[:, n, :],
+                        rhs=w_codes[:, g, first : first + width].bitcast(FP8X4),
+                        rhs_scale=w_scales[:, g, first : first + width],
+                        start=(n == 0),
+                        stop=(n == ITEMS - 1),
+                    )
 
         result = keep.tile([P, H], F32)
 
@@ -192,52 +202,55 @@ def tile_declayerj_pb_kernel(tc, h2, h_V, mask_attend, W3_w, W3_b, out):
             )
             nc.sync.dma_start(out=out_rows[:, cols], in_=result[:, cols])
 
-        def edges_of(first):
-            return range(first, first + RUN)
+        def spin(times):
+            spun = turn_pool.tile([P, N_HALF], F32, tag="turn")
+            for i in range(times):
+                nc.tensor.matmul(out=spun[:], lhsT=ones[:], rhs=blank[:], start=True, stop=True)
 
-        def multiply_all(g, groups, first):
-            for group in groups:
-                multiply(g, group, edges_of(first))
-
-        every, early, late = range(len(GROUPS)), range(LATE), range(LATE, len(GROUPS))
-        spread_bias()
+        every, late = (0, 1, 2), (1, 2)
+        spin(6)
         regroup_w(0, 0)
         quantise_w(0, 0)
-        turn_h2(0, 0)
-        quantise_h2(0, 0, PAIR)
-        regroup_w(0, 256)
-        quantise_w(0, 256)
-        quantise_h2(0, PAIR, PAIR)
-        multiply_all(0, early, 0)
-        regroup_w(0, 512)
-        quantise_w(0, 512)
+        make_gates(8, 16)
+        planes_of(0, False)
         turn_h2(0, 4)
         quantise_h2(0, 4)
-        make_late_gates()
-        multiply_all(0, late, 0)
-        turn_h2(0, 8)
-        quantise_h2(0, 8)
+        spin(2)
+        spread_bias()
+        planes_of(4, True)
+        planes_of(8, True)
+        multiply((0,), 0, 4)
+        turn_h2(4, 12)
+        regroup_w(0, 512)
+        quantise_w(0, 512)
+        quantise_h2(4, 12)
+        planes_of(12, True)
+        planes_of(16, True)
+        multiply(late, 0, 4)
+        multiply(every, 4, 8)
+        turn_h2(12, 20)
         regroup_w(1, 0)
-        multiply_all(0, every, 4)
-        turn_h2(0, 12)
-        quantise_h2(0, 12)
+        quantise_h2(12, 20)
         quantise_w(1, 0)
+        planes_of(20, True)
+        planes_of(24, True)
+        multiply(every, 8, 16)
+        turn_h2(20, 28)
+        planes_of(28, True)
+        quantise_h2(20, 28)
         regroup_w(1, 512)
-        multiply_all(0, every, 8)
-        turn_h2(1, 0)
-        quantise_h2(1, 0)
         quantise_w(1, 512)
-        multiply_all(0, every, 12)
-        for first in range(RUN, EDGES, RUN):
-            turn_h2(1, first)
-            quantise_h2(1, first)
-            multiply_all(1, early, first - RUN)
-        multiply_all(1, early, EDGES - RUN)
+        multiply((0,), 16, 24)
+        turn_h2(28, 32)
+        quantise_h2(28, 32)
+        multiply((0,), 24, 28)
+        multiply((1,), 16, 20)
+        multiply((0,), 28, 32)
         for half in range(HALVES):
             cols = slice(N_HALF * half, N_HALF * (half + 1))
             nc.vector.tensor_tensor(out=base[:, cols], in0=base[:, cols], in1=hv[:, cols], op=ALU.add)
-        for group in early:
-            finish(group)
-        for group in late:
-            multiply(1, group, range(EDGES))
-            finish(group)
+        finish(0)
+        multiply((1,), 20, 32)
+        finish(1)
+        multiply((2,), 16, 32)
+        finish(2)

@@ -77,8 +77,8 @@ def tile_declayerj_pb_kernel(tc, h2, h_V, mask_attend, W3_w, W3_b, out):
         load_h2(4, 4)
         load_h2(8, 4)
         load_h2(12, 4)
-        load_w(1, 0, 512)
         load_h2(16, 4)
+        load_w(1, 0, 512)
         load_h2(20, 4)
         load_h2(24, 4)
         load_w(1, 512, 512)
@@ -99,6 +99,8 @@ def tile_declayerj_pb_kernel(tc, h2, h_V, mask_attend, W3_w, W3_b, out):
                 )
 
         make_gates(0, 8)
+        for e in range(8, EDGES):
+            nc.scalar.activation(out=gates[:, e, :], in_=ident[:], func=ACT.Copy, scale=mask_f32[:, e : e + 1])
 
         count = keep.tile([P, 1], F32)
         nc.vector.reduce_sum(out=count[:], in_=mask_f32[:], axis=mybir.AxisListType.X)
@@ -118,12 +120,12 @@ def tile_declayerj_pb_kernel(tc, h2, h_V, mask_attend, W3_w, W3_b, out):
         w_scales = keep.tile([P, HALVES, H], U8, align_bytes=64)
         w_grouped = {}
 
-        def regroup_w(g, first):
+        def regroup_w(g, first, copy):
             raw = w_raw[g, first]
             width = raw.shape[2]
             grouped = keep.tile([P, width, PACK], BF16, name="w_grouped%d_%d" % (g, first), align_bytes=64)
             w_grouped[g, first] = grouped
-            nc.vector.tensor_copy(
+            copy(
                 out=grouped[:].rearrange("p (c i) t -> p c t i", i=4),
                 in_=raw[:].rearrange("p t (c i) -> p c t i", i=4),
             )
@@ -139,7 +141,7 @@ def tile_declayerj_pb_kernel(tc, h2, h_V, mask_attend, W3_w, W3_b, out):
 
         h2_codes = keep.tile([P, ITEMS, P], U32, align_bytes=64)
         h2_scales = keep.tile([P, ITEMS, P], U8, align_bytes=64)
-        h2_grouped = {}
+        h2_grouped = keep.tile([P, ITEMS, P * PACK], BF16, align_bytes=64)
 
         planes = {}
 
@@ -160,19 +162,17 @@ def tile_declayerj_pb_kernel(tc, h2, h_V, mask_attend, W3_w, W3_b, out):
                     gate = gates[:, (pair + i) % EDGES, :]
                     for u in range(2):
                         nc.tensor.transpose(turned[:, i, u, :], planes[pair + i][u], gate)
-                grouped = keep.tile([P, PAIR * P * PACK], BF16, name="h2_grouped%d" % pair, align_bytes=64)
                 nc.scalar.copy(
-                    out=grouped[:].bitcast(F32).rearrange("p (i n u) -> p i n u", i=PAIR, u=2),
+                    out=h2_grouped[:, pair : pair + PAIR, :].bitcast(F32).rearrange("p i (n u) -> p i n u", u=2),
                     in_=turned[:].rearrange("p i u n -> p i n u"),
                 )
-                h2_grouped[pair] = grouped
 
-        def quantise_h2(first, end):
-            for pair in range(first, end, PAIR):
+        def quantise_h2(first, end, items):
+            for n in range(first, end, items):
                 nc.vector.quantize_mx(
-                    out=h2_codes[:, pair : pair + PAIR, :].rearrange("p i n -> p (i n)").bitcast(FP8X4),
-                    scales=h2_scales[:, pair : pair + PAIR, :].rearrange("p i n -> p (i n)"),
-                    in_=h2_grouped[pair][:],
+                    out=h2_codes[:, n : n + items, :].rearrange("p i n -> p (i n)").bitcast(FP8X4),
+                    scales=h2_scales[:, n : n + items, :].rearrange("p i n -> p (i n)"),
+                    in_=h2_grouped[:, n : n + items, :].rearrange("p i k -> p (i k)"),
                 )
 
         acc = [acc_pool.tile([P, width], F32, name="acc%d" % i) for i, (first, width) in enumerate(GROUPS)]
@@ -208,49 +208,45 @@ def tile_declayerj_pb_kernel(tc, h2, h_V, mask_attend, W3_w, W3_b, out):
                 nc.tensor.matmul(out=spun[:], lhsT=ones[:], rhs=blank[:], start=True, stop=True)
 
         every, late = (0, 1, 2), (1, 2)
-        spin(6)
-        regroup_w(0, 0)
+        spin(8)
+        regroup_w(0, 0, nc.vector.tensor_copy)
         quantise_w(0, 0)
-        make_gates(8, 16)
         planes_of(0, False)
+        planes_of(4, False)
         turn_h2(0, 4)
-        quantise_h2(0, 4)
-        spin(2)
+        quantise_h2(0, 4, PAIR)
         spread_bias()
-        planes_of(4, True)
-        planes_of(8, True)
-        multiply((0,), 0, 4)
-        turn_h2(4, 12)
-        regroup_w(0, 512)
+        regroup_w(0, 512, nc.vector.tensor_copy)
         quantise_w(0, 512)
-        quantise_h2(4, 12)
+        multiply((0,), 0, 4)
+        turn_h2(4, 8)
+        planes_of(8, True)
         planes_of(12, True)
-        planes_of(16, True)
+        quantise_h2(4, 8, 4)
         multiply(late, 0, 4)
-        multiply(every, 4, 8)
-        turn_h2(12, 20)
-        regroup_w(1, 0)
-        quantise_h2(12, 20)
-        quantise_w(1, 0)
+        turn_h2(8, 16)
+        quantise_h2(8, 16, 4)
+        planes_of(16, True)
+        regroup_w(1, 0, nc.scalar.copy)
+        multiply(every, 4, 12)
         planes_of(20, True)
+        turn_h2(16, 24)
+        quantise_w(1, 0)
+        quantise_h2(16, 24, 4)
         planes_of(24, True)
-        multiply(every, 8, 16)
-        turn_h2(20, 28)
         planes_of(28, True)
-        quantise_h2(20, 28)
-        regroup_w(1, 512)
+        regroup_w(1, 512, nc.scalar.copy)
+        multiply(every, 12, 16)
+        multiply((0,), 16, 20)
+        turn_h2(24, 32)
         quantise_w(1, 512)
-        multiply((0,), 16, 24)
-        turn_h2(28, 32)
-        quantise_h2(28, 32)
-        multiply((0,), 24, 28)
-        multiply((1,), 16, 20)
-        multiply((0,), 28, 32)
-        for half in range(HALVES):
-            cols = slice(N_HALF * half, N_HALF * (half + 1))
-            nc.vector.tensor_tensor(out=base[:, cols], in0=base[:, cols], in1=hv[:, cols], op=ALU.add)
+        quantise_h2(24, 32, 4)
+        multiply((0,), 20, 24)
+        multiply((1,), 16, 24)
+        multiply((0,), 24, 32)
+        nc.vector.tensor_tensor(out=base[:], in0=base[:], in1=hv[:], op=ALU.add)
         finish(0)
-        multiply((1,), 20, 32)
+        multiply((1,), 24, 32)
         finish(1)
         multiply((2,), 16, 32)
         finish(2)

@@ -72,9 +72,10 @@ def tile_declayerj_pb_kernel(tc, h2, h_V, mask_attend, W3_w, W3_b, out):
             )
 
         load_w(0, 0, 512)
-        load_h2(0, 4)
-        load_w(0, 512, 512)
+        load_h2(0, 2)
+        load_h2(2, 2)
         load_h2(4, 4)
+        load_w(0, 512, 512)
         load_h2(8, 4)
         load_h2(12, 4)
         load_h2(16, 4)
@@ -99,8 +100,6 @@ def tile_declayerj_pb_kernel(tc, h2, h_V, mask_attend, W3_w, W3_b, out):
                 )
 
         make_gates(0, 8)
-        for e in range(8, EDGES):
-            nc.scalar.activation(out=gates[:, e, :], in_=ident[:], func=ACT.Copy, scale=mask_f32[:, e : e + 1])
 
         count = keep.tile([P, 1], F32)
         nc.vector.reduce_sum(out=count[:], in_=mask_f32[:], axis=mybir.AxisListType.X)
@@ -109,25 +108,30 @@ def tile_declayerj_pb_kernel(tc, h2, h_V, mask_attend, W3_w, W3_b, out):
 
         base = keep.tile([P, H], F32)
 
+        spread = [acc_pool.tile([P, N_HALF], F32, name="spread%d" % half, tag="acc%d" % (half + 1)) for half in range(HALVES)]
+
         def spread_bias():
             for half in range(HALVES):
                 cols = slice(N_HALF * half, N_HALF * (half + 1))
-                spread = turn_pool.tile([P, N_HALF], F32, tag="turn")
-                nc.tensor.matmul(out=spread[:], lhsT=ones[:], rhs=bias_rows[:, cols], start=True, stop=True)
-                nc.scalar.activation(out=base[:, cols], in_=spread[:], func=ACT.Copy, scale=count30[:, 0:1])
+                nc.tensor.matmul(out=spread[half][:], lhsT=ones[:], rhs=bias_rows[:, cols], start=True, stop=True)
+
+        def scale_bias():
+            for half in range(HALVES):
+                cols = slice(N_HALF * half, N_HALF * (half + 1))
+                nc.scalar.activation(out=base[:, cols], in_=spread[half][:], func=ACT.Copy, scale=count30[:, 0:1])
 
         w_codes = keep.tile([P, HALVES, H], U32, align_bytes=64)
         w_scales = keep.tile([P, HALVES, H], U8, align_bytes=64)
         w_grouped = {}
 
-        def regroup_w(g, first, copy):
-            raw = w_raw[g, first]
-            width = raw.shape[2]
+        def regroup_w(g, first, width, copy):
+            half = first // N_HALF
+            start = first % N_HALF
             grouped = keep.tile([P, width, PACK], BF16, name="w_grouped%d_%d" % (g, first), align_bytes=64)
             w_grouped[g, first] = grouped
             copy(
                 out=grouped[:].rearrange("p (c i) t -> p c t i", i=4),
-                in_=raw[:].rearrange("p t (c i) -> p c t i", i=4),
+                in_=w_raw[g, N_HALF * half][:, :, start : start + width].rearrange("p t (c i) -> p c t i", i=4),
             )
 
         def quantise_w(g, first):
@@ -175,7 +179,7 @@ def tile_declayerj_pb_kernel(tc, h2, h_V, mask_attend, W3_w, W3_b, out):
                     in_=h2_grouped[:, n : n + items, :].rearrange("p i k -> p (i k)"),
                 )
 
-        acc = [acc_pool.tile([P, width], F32, name="acc%d" % i) for i, (first, width) in enumerate(GROUPS)]
+        acc = [acc_pool.tile([P, width], F32, name="acc%d" % i, tag="acc%d" % i) for i, (first, width) in enumerate(GROUPS)]
 
         def multiply(groups, items_first, items_end):
             for group in groups:
@@ -208,34 +212,43 @@ def tile_declayerj_pb_kernel(tc, h2, h_V, mask_attend, W3_w, W3_b, out):
                 nc.tensor.matmul(out=spun[:], lhsT=ones[:], rhs=blank[:], start=True, stop=True)
 
         every, late = (0, 1, 2), (1, 2)
-        spin(8)
-        regroup_w(0, 0, nc.vector.tensor_copy)
+        spin(6)
+        spread_bias()
+        regroup_w(0, 0, 256, nc.vector.tensor_copy)
+        regroup_w(0, 256, 256, nc.scalar.copy)
+        make_gates(8, 16)
         quantise_w(0, 0)
+        quantise_w(0, 256)
         planes_of(0, False)
+        planes_of(2, False)
         planes_of(4, False)
         turn_h2(0, 4)
         quantise_h2(0, 4, PAIR)
-        spread_bias()
-        regroup_w(0, 512, nc.vector.tensor_copy)
-        quantise_w(0, 512)
-        multiply((0,), 0, 4)
+        spin(2)
         turn_h2(4, 8)
+        regroup_w(0, 512, 256, nc.vector.tensor_copy)
+        quantise_h2(4, 8, PAIR)
+        multiply((0,), 0, 8)
+        scale_bias()
+        regroup_w(0, 768, 256, nc.scalar.copy)
+        quantise_w(0, 512)
         planes_of(8, True)
         planes_of(12, True)
-        quantise_h2(4, 8, 4)
-        multiply(late, 0, 4)
+        quantise_w(0, 768)
+        multiply((1,), 0, 8)
         turn_h2(8, 16)
-        quantise_h2(8, 16, 4)
+        quantise_h2(8, 16, PAIR)
         planes_of(16, True)
-        regroup_w(1, 0, nc.scalar.copy)
-        multiply(every, 4, 12)
+        regroup_w(1, 0, 512, nc.scalar.copy)
+        multiply((2,), 0, 8)
+        multiply(every, 8, 12)
         planes_of(20, True)
         turn_h2(16, 24)
         quantise_w(1, 0)
         quantise_h2(16, 24, 4)
         planes_of(24, True)
         planes_of(28, True)
-        regroup_w(1, 512, nc.scalar.copy)
+        regroup_w(1, 512, 512, nc.scalar.copy)
         multiply(every, 12, 16)
         multiply((0,), 16, 20)
         turn_h2(24, 32)

@@ -47,8 +47,7 @@ def tile_declayerj_pb_kernel(tc, h2, h_V, mask_attend, W3_w, W3_b, out):
         blank = keep.tile([P, N_HALF], BF16)
         nc.vector.memset(blank[:].bitcast(F32), 0.0)
         mask_bf = keep.tile([P, EDGES], BF16)
-        nc.scalar.dma_start(out=mask_bf[:], in_=mask_rows)
-        nc.scalar.dma_start(out=bias_rows[0:1, :], in_=W3_b.unsqueeze(0))
+        nc.sync.dma_start(out=mask_bf[:], in_=mask_rows)
         warm = keep.tile([P, 1], F32)
         nc.scalar.copy(out=warm[:], in_=ones[:, 0:1])
 
@@ -73,6 +72,7 @@ def tile_declayerj_pb_kernel(tc, h2, h_V, mask_attend, W3_w, W3_b, out):
 
         load_w(0, 0, 512)
         load_h2(0, 2)
+        nc.sync.dma_start(out=bias_rows[0:1, :], in_=W3_b.unsqueeze(0))
         load_h2(2, 2)
         load_h2(4, 4)
         load_w(0, 512, 512)
@@ -108,11 +108,12 @@ def tile_declayerj_pb_kernel(tc, h2, h_V, mask_attend, W3_w, W3_b, out):
 
         base = keep.tile([P, H], F32)
 
-        spread = [acc_pool.tile([P, N_HALF], F32, name="spread%d" % half, tag="acc%d" % (half + 1)) for half in range(HALVES)]
+        spread = {}
 
         def spread_bias():
             for half in range(HALVES):
                 cols = slice(N_HALF * half, N_HALF * (half + 1))
+                spread[half] = turn_pool.tile([P, N_HALF], F32, name="spread%d" % half, tag="turn")
                 nc.tensor.matmul(out=spread[half][:], lhsT=ones[:], rhs=bias_rows[:, cols], start=True, stop=True)
 
         def scale_bias():
@@ -212,8 +213,7 @@ def tile_declayerj_pb_kernel(tc, h2, h_V, mask_attend, W3_w, W3_b, out):
                 nc.tensor.matmul(out=spun[:], lhsT=ones[:], rhs=blank[:], start=True, stop=True)
 
         every, late = (0, 1, 2), (1, 2)
-        spin(6)
-        spread_bias()
+        spin(7)
         regroup_w(0, 0, 256, nc.vector.tensor_copy)
         regroup_w(0, 256, 256, nc.scalar.copy)
         make_gates(8, 16)
@@ -224,35 +224,39 @@ def tile_declayerj_pb_kernel(tc, h2, h_V, mask_attend, W3_w, W3_b, out):
         planes_of(4, False)
         turn_h2(0, 4)
         quantise_h2(0, 4, PAIR)
-        spin(2)
+        spread_bias()
         turn_h2(4, 8)
         regroup_w(0, 512, 256, nc.vector.tensor_copy)
-        quantise_h2(4, 8, PAIR)
-        multiply((0,), 0, 8)
-        scale_bias()
         regroup_w(0, 768, 256, nc.scalar.copy)
+        quantise_h2(4, 8, PAIR)
+        scale_bias()
+        multiply((0,), 0, 8)
         quantise_w(0, 512)
         planes_of(8, True)
-        planes_of(12, True)
         quantise_w(0, 768)
+        planes_of(12, True)
         multiply((1,), 0, 8)
         turn_h2(8, 16)
         quantise_h2(8, 16, PAIR)
         planes_of(16, True)
-        regroup_w(1, 0, 512, nc.scalar.copy)
+        planes_of(20, True)
+        regroup_w(1, 0, 256, nc.scalar.copy)
+        regroup_w(1, 256, 256, nc.scalar.copy)
         multiply((2,), 0, 8)
         multiply(every, 8, 12)
-        planes_of(20, True)
         turn_h2(16, 24)
         quantise_w(1, 0)
+        quantise_w(1, 256)
         quantise_h2(16, 24, 4)
         planes_of(24, True)
         planes_of(28, True)
-        regroup_w(1, 512, 512, nc.scalar.copy)
+        regroup_w(1, 512, 256, nc.scalar.copy)
+        regroup_w(1, 768, 256, nc.vector.tensor_copy)
         multiply(every, 12, 16)
         multiply((0,), 16, 20)
         turn_h2(24, 32)
         quantise_w(1, 512)
+        quantise_w(1, 768)
         quantise_h2(24, 32, 4)
         multiply((0,), 20, 24)
         multiply((1,), 16, 24)

from contextlib import ExitStack

import concourse.mybir as mybir
from concourse.masks import make_identity

F32 = mybir.dt.float32
BF16 = mybir.dt.bfloat16
U32 = mybir.dt.uint32
U8 = mybir.dt.uint8
FP8X4 = mybir.dt.float8_e4m3fn_x4
ALU = mybir.AluOpType
ACT = mybir.ActivationFunctionType

P = 128
EDGES = 16
K = 1024
H = 1024
PACK = 4
K_HALF = P * PACK
HALVES = 2
N_HALF = H // HALVES
GROUPS = ((0, 512), (512, 256), (768, 256))
ITEMS = HALVES * EDGES
PAIR = 2
SCALE = 30.0

FLOPS = 2 * P * EDGES * K * H


def tile_declayerj_pb_kernel(tc, h2, h_V, mask_attend, W3_w, W3_b, out):
    nc = tc.nc
    h2_rows = h2.rearrange("b n e k -> (b n) e k")
    mask_rows = mask_attend.rearrange("b n e -> (b n) e")
    hv_rows = h_V.rearrange("b n h -> (b n) h")
    out_rows = out.rearrange("b n h -> (b n) h")

    with ExitStack() as ctx:
        keep = ctx.enter_context(tc.tile_pool(name="keep", bufs=1))
        acc_pool = ctx.enter_context(tc.psum_pool(name="acc", bufs=1))
        turn_pool = ctx.enter_context(tc.psum_pool(name="turn", bufs=5))
        ctx.enter_context(tc.manual_schedule())

        bias_rows = keep.tile([P, H], BF16)
        nc.gpsimd.memset(bias_rows[:].bitcast(F32), 0.0)
        ones = keep.tile([P, P], BF16)
        nc.vector.memset(ones[:], 1.0)
        blank = keep.tile([P, N_HALF], BF16)
        nc.vector.memset(blank[:].bitcast(F32), 0.0)
        mask_bf = keep.tile([P, EDGES], BF16)
        nc.sync.dma_start(out=mask_bf[:], in_=mask_rows)
        warm = keep.tile([P, 1], F32)
        nc.scalar.copy(out=warm[:], in_=ones[:, 0:1])

        w_raw = {}
        h2_in = {}

        def load_w(g, first, width):
            w_raw[g, first] = keep.tile([P, PACK, width], BF16, name="w_raw%d_%d" % (g, first))
            nc.sync.dma_start(
                out=w_raw[g, first][:],
                in_=W3_w[K_HALF * g : K_HALF * (g + 1), first : first + width].rearrange("(p t) c -> p t c", t=PACK),
            )

        def load_h2(first, items):
            piece = keep.tile([P, items, K_HALF], BF16, name="h2_in%d" % first)
            h2_in[first] = piece
            g, e = divmod(first, EDGES)
            nc.sync.dma_start(
                out=piece[:],
                in_=h2_rows[:, e : e + items, K_HALF * g : K_HALF * (g + 1)],
            )

        load_w(0, 0, 512)
        load_h2(0, 2)
        nc.sync.dma_start(out=bias_rows[0:1, :], in_=W3_b.unsqueeze(0))
        load_h2(2, 2)
        load_h2(4, 4)
        load_w(0, 512, 512)
        load_h2(8, 4)
        load_h2(12, 4)
        load_h2(16, 4)
        load_w(1, 0, 512)
        load_h2(20, 4)
        load_h2(24, 4)
        load_w(1, 512, 512)
        load_h2(28, 4)
        hv = keep.tile([P, H], BF16)
        nc.sync.dma_start(out=hv[:], in_=hv_rows)

        ident = keep.tile([P, P], F32)
        make_identity(nc, ident[:])
        mask_f32 = keep.tile([P, EDGES], F32)
        nc.vector.tensor_copy(out=mask_f32[:], in_=mask_bf[:])
        gates = keep.tile([P, EDGES, P], F32)

        def make_gates(first, end):
            for e in range(first, end):
                nc.vector.tensor_scalar(
                    out=gates[:, e, :], in0=ident[:], scalar1=mask_f32[:, e : e + 1], scalar2=None, op0=ALU.mult
                )

        make_gates(0, 8)

        count = keep.tile([P, 1], F32)
        nc.vector.reduce_sum(out=count[:], in_=mask_f32[:], axis=mybir.AxisListType.X)
        count30 = keep.tile([P, 1], F32)
        nc.vector.tensor_scalar(out=count30[:], in0=count[:], scalar1=1.0 / SCALE, scalar2=None, op0=ALU.mult)

        base = keep.tile([P, H], F32)

        spread = {}

        def spread_bias():
            for half in range(HALVES):
                cols = slice(N_HALF * half, N_HALF * (half + 1))
                spread[half] = turn_pool.tile([P, N_HALF], F32, name="spread%d" % half, tag="turn")
                nc.tensor.matmul(out=spread[half][:], lhsT=ones[:], rhs=bias_rows[:, cols], start=True, stop=True)

        def scale_bias():
            for half in range(HALVES):
                cols = slice(N_HALF * half, N_HALF * (half + 1))
                nc.scalar.activation(out=base[:, cols], in_=spread[half][:], func=ACT.Copy, scale=count30[:, 0:1])

        w_codes = keep.tile([P, HALVES, H], U32, align_bytes=64)
        w_scales = keep.tile([P, HALVES, H], U8, align_bytes=64)
        w_grouped = {}

        def regroup_w(g, first, width, copy):
            half = first // N_HALF
            start = first % N_HALF
            grouped = keep.tile([P, width, PACK], BF16, name="w_grouped%d_%d" % (g, first), align_bytes=64)
            w_grouped[g, first] = grouped
            copy(
                out=grouped[:].rearrange("p (c i) t -> p c t i", i=4),
                in_=w_raw[g, N_HALF * half][:, :, start : start + width].rearrange("p t (c i) -> p c t i", i=4),
            )

        def quantise_w(g, first):
            grouped = w_grouped[g, first]
            cols = slice(first, first + grouped.shape[1])
            nc.vector.quantize_mx(
                out=w_codes[:, g, cols].bitcast(FP8X4),
                scales=w_scales[:, g, cols],
                in_=grouped[:].rearrange("p c t -> p (c t)"),
            )

        h2_codes = keep.tile([P, ITEMS, P], U32, align_bytes=64)
        h2_scales = keep.tile([P, ITEMS, P], U8, align_bytes=64)
        h2_grouped = keep.tile([P, ITEMS, P * PACK], BF16, align_bytes=64)

        planes = {}

        def planes_of(first, order):
            words = h2_in[first][:].bitcast(F32).rearrange("p i (n u) -> p i u n", u=2)
            items = words.shape[1]
            if order:
                ordered = keep.tile([P, items, 2, P], F32, name="h2_ordered%d" % first)
                nc.vector.tensor_copy(out=ordered[:], in_=words)
                words = ordered[:]
            for i in range(items):
                planes[first + i] = [words[:, i, u, :] for u in range(2)]

        def turn_h2(first, end):
            for pair in range(first, end, PAIR):
                turned = turn_pool.tile([P, PAIR, 2, P], F32, tag="turn")
                for i in range(PAIR):
                    gate = gates[:, (pair + i) % EDGES, :]
                    for u in range(2):
                        nc.tensor.transpose(turned[:, i, u, :], planes[pair + i][u], gate)
                nc.scalar.copy(
                    out=h2_grouped[:, pair : pair + PAIR, :].bitcast(F32).rearrange("p i (n u) -> p i n u", u=2),
                    in_=turned[:].rearrange("p i u n -> p i n u"),
                )

        def quantise_h2(first, end, items):
            for n in range(first, end, items):
                nc.vector.quantize_mx(
                    out=h2_codes[:, n : n + items, :].rearrange("p i n -> p (i n)").bitcast(FP8X4),
                    scales=h2_scales[:, n : n + items, :].rearrange("p i n -> p (i n)"),
                    in_=h2_grouped[:, n : n + items, :].rearrange("p i k -> p (i k)"),
                )

        acc = [acc_pool.tile([P, width], F32, name="acc%d" % i, tag="acc%d" % i) for i, (first, width) in enumerate(GROUPS)]

        def multiply(groups, items_first, items_end):
            for group in groups:
                first, width = GROUPS[group]
                for n in range(items_first, items_end):
                    g = n // EDGES
                    nc.tensor.matmul_mx(
                        out=acc[group][:],
                        lhsT=h2_codes[:, n, :].bitcast(FP8X4),
                        lhsT_scale=h2_scales[:, n, :],
                        rhs=w_codes[:, g, first : first + width].bitcast(FP8X4),
                        rhs_scale=w_scales[:, g, first : first + width],
                        start=(n == 0),
                        stop=(n == ITEMS - 1),
                    )

        result = keep.tile([P, H], F32)

        def finish(group):
            first, width = GROUPS[group]
            cols = slice(first, first + width)
            nc.vector.scalar_tensor_tensor(
                out=result[:, cols], in0=acc[group][:], scalar=1.0 / SCALE, in1=base[:, cols], op0=ALU.mult, op1=ALU.add
            )
            nc.sync.dma_start(out=out_rows[:, cols], in_=result[:, cols])

        def spin(times):
            spun = turn_pool.tile([P, N_HALF], F32, tag="turn")
            for i in range(times):
                nc.tensor.matmul(out=spun[:], lhsT=ones[:], rhs=blank[:], start=True, stop=True)

        every, late = (0, 1, 2), (1, 2)
        spin(7)
        regroup_w(0, 0, 256, nc.vector.tensor_copy)
        regroup_w(0, 256, 256, nc.scalar.copy)
        make_gates(8, 16)
        quantise_w(0, 0)
        quantise_w(0, 256)
        planes_of(0, False)
        planes_of(2, False)
        planes_of(4, False)
        turn_h2(0, 4)
        quantise_h2(0, 4, PAIR)
        spread_bias()
        turn_h2(4, 8)
        regroup_w(0, 512, 256, nc.vector.tensor_copy)
        regroup_w(0, 768, 256, nc.scalar.copy)
        quantise_h2(4, 8, PAIR)
        scale_bias()
        multiply((0,), 0, 8)
        quantise_w(0, 512)
        planes_of(8, True)
        quantise_w(0, 768)
        planes_of(12, True)
        multiply((1,), 0, 8)
        turn_h2(8, 16)
        quantise_h2(8, 16, PAIR)
        planes_of(16, True)
        planes_of(20, True)
        regroup_w(1, 0, 256, nc.scalar.copy)
        regroup_w(1, 256, 256, nc.scalar.copy)
        multiply((2,), 0, 8)
        multiply(every, 8, 12)
        turn_h2(16, 24)
        quantise_w(1, 0)
        quantise_w(1, 256)
        quantise_h2(16, 24, 4)
        planes_of(24, True)
        planes_of(28, True)
        regroup_w(1, 512, 256, nc.scalar.copy)
        regroup_w(1, 768, 256, nc.vector.tensor_copy)
        multiply(every, 12, 16)
        multiply((0,), 16, 20)
        turn_h2(24, 32)
        quantise_w(1, 512)
        quantise_w(1, 768)
        quantise_h2(24, 32, 4)
        multiply((0,), 20, 24)
        multiply((1,), 16, 24)
        multiply((0,), 24, 32)
        nc.vector.tensor_tensor(out=base[:], in0=base[:], in1=hv[:], op=ALU.add)
        finish(0)
        multiply((1,), 24, 32)
        finish(1)
        multiply((2,), 16, 32)
        finish(2)
